import numpy as np
import ml_dtypes


def mxq(x, axis, fmt="e4m3"):
    dtype, down = {"e4m3": (ml_dtypes.float8_e4m3fn, 7), "e5m2": (ml_dtypes.float8_e5m2, 14)}[fmt]
    v = np.moveaxis(np.asarray(x, np.float32).astype(ml_dtypes.bfloat16).astype(np.float64), axis, -1)
    blocks = v.reshape(v.shape[:-1] + (-1, 32))
    amax = np.abs(blocks).max(-1, keepdims=True)
    byte = np.maximum(np.where(amax > 0, np.frexp(amax)[1] - 1 + 127, 0) - down, 1)
    scale = np.exp2(byte - 127.0)
    codes = (blocks / scale).astype(np.float32).astype(dtype).astype(np.float64)
    return np.moveaxis((codes * scale).reshape(v.shape), -1, axis)


WIDE = False


def mx_kscale(k):
    if not WIDE:
        return np.ones(k)
    levels = np.array([10, -10, 5, -5, 0])
    a = np.random.permutation(np.resize(levels, k // 512 * 4)).reshape(k // 512, 4)
    idx = np.arange(k)
    return np.exp2(a[idx // 512, idx % 128 // 32])


BF16 = ml_dtypes.bfloat16


def bf(x):
    return np.asarray(x, np.float32).astype(BF16)


def f64(x):
    return np.asarray(x).astype(np.float64)


B, S, A, O, H, L = 1024, 1024, 128, 1920, 1024, 384
K1 = S + A + O


def setup_inputs():
    s = mx_kscale(K1)
    t = mx_kscale(H)
    col = np.concatenate([np.full(L, 0.7), np.full(L, 0.14)]) / np.sqrt(H)
    return {"prev_state": bf(np.random.standard_normal((B, S)) * s[:S]),
            "prev_action": bf(np.random.standard_normal((B, A)) * s[S:S + A]),
            "observation": bf(np.random.standard_normal((B, O)) * s[S + A:]),
            "eps": bf(np.random.standard_normal((B, L))),
            "rep_W1": bf(np.random.standard_normal((K1, H)) / np.sqrt(K1) / s[:, None] * t),
            "rep_b1": bf(np.random.standard_normal(H) * 0.1 * t),
            "rep_W2": bf(np.random.standard_normal((H, 2 * L)) * col / t[:, None]),
            "rep_b2": bf(np.concatenate([0.1 * np.random.standard_normal(L), 1.0 + 0.1 * np.random.standard_normal(L)]))}


def reference(prev_state, prev_action, observation, eps, rep_W1, rep_b1, rep_W2, rep_b2):
    x = np.concatenate([f64(prev_state), f64(prev_action), f64(observation)], axis=-1)
    h1 = np.maximum((mxq(x, 1, "e4m3") @ mxq(f64(rep_W1), 0, "e4m3")) + f64(rep_b1), 0.0)
    out = (mxq(h1, 1, "e4m3") @ mxq(f64(rep_W2), 0, "e4m3")) + f64(rep_b2)
    mean, std = np.split(out, 2, axis=-1)
    sample = mean + np.sqrt(std) * f64(eps)
    return mean, std, sample

@@ -1,0 +1,329 @@
+from contextlib import ExitStack
+
+import concourse.mybir as mybir
+from concourse.masks import make_identity
+
+F32 = mybir.dt.float32
+BF16 = mybir.dt.bfloat16
+U32 = mybir.dt.uint32
+U8 = mybir.dt.uint8
+FP8X4 = mybir.dt.float8_e4m3fn_x4
+ACT = mybir.ActivationFunctionType
+ALU = mybir.AluOpType
+
+P = 128
+PACK = 4
+K_PASS = P * PACK
+
+BATCH, STATE, ACTION, OBS, HIDDEN, LATENT = 1024, 1024, 128, 1920, 1024, 384
+K1 = STATE + ACTION + OBS
+OUT = 2 * LATENT
+PASSES1 = K1 // K_PASS
+PASSES2 = HIDDEN // K_PASS
+
+HALF = 512
+HALVES = BATCH // HALF
+SUB = HALF // P
+X_CHUNK = 2 * K_PASS
+CHUNKS = K1 // X_CHUNK
+WORDS = K_PASS // 2
+
+H_TILES = HIDDEN // P
+LOW = (0, 1, 2, 3)
+HIGH = (4, 5, 6, 7)
+
+OUT_BANKS = ((0, HALF), (HALF, OUT))
+
+VECTOR_SHARE_16THS = 9
+
+FLOPS = 2 * BATCH * K1 * HIDDEN + 2 * BATCH * HIDDEN * OUT
+
+
+def tile_rssm_pa_kernel(
+    tc, prev_state, prev_action, observation, eps, rep_W1, rep_b1, rep_W2, rep_b2, out_0, out_1, out_2
+):
+    nc = tc.nc
+    with ExitStack() as ctx:
+        ctx.enter_context(tc.manual_schedule())
+        keep = ctx.enter_context(tc.tile_pool(name="keep", bufs=1))
+        x_raw_pool = ctx.enter_context(tc.tile_pool(name="x_raw", bufs=3))
+        x_grp_pool = ctx.enter_context(tc.tile_pool(name="x_grp", bufs=4))
+        w_raw_pool = ctx.enter_context(tc.tile_pool(name="w_raw", bufs=4))
+        w_grp_pool = ctx.enter_context(tc.tile_pool(name="w_grp", bufs=2))
+        hidden_pool = ctx.enter_context(tc.tile_pool(name="hidden", bufs=2))
+        result_pool = ctx.enter_context(tc.tile_pool(name="result", bufs=3))
+        psum = ctx.enter_context(tc.psum_pool(name="psum", bufs=4))
+
+        def by_tile(dram):
+            return dram.rearrange("(h p t) c -> h p t c", h=HALVES, t=SUB)
+
+        x_sources = ((by_tile(prev_state), 0), (by_tile(prev_action), STATE), (by_tile(observation), STATE + ACTION))
+        outputs = (by_tile(out_0), by_tile(out_1), by_tile(out_2))
+
+        x_codes = keep.tile([P, HALVES, PASSES1, HALF], U32, align_bytes=64)
+        x_scales = keep.tile([P, HALVES, PASSES1, HALF], U8, align_bytes=64)
+        w1_codes = keep.tile([P, PASSES1, HIDDEN], U32, align_bytes=64)
+        w1_scales = keep.tile([P, PASSES1, HIDDEN], U8, align_bytes=64)
+        h1_codes = keep.tile([P, PASSES2, BATCH], U32, align_bytes=64)
+        h1_scales = keep.tile([P, PASSES2, BATCH], U8, align_bytes=64)
+        w2_codes = keep.tile([P, PASSES2, OUT], U32, align_bytes=64)
+        w2_scales = keep.tile([P, PASSES2, OUT], U8, align_bytes=64)
+
+        def load_x(half, chunk):
+            raw = x_raw_pool.tile([P, SUB * X_CHUNK], BF16, name="x_raw")
+            rows = raw[:].rearrange("p (t k) -> p t k", t=SUB)
+            first = chunk * X_CHUNK
+            for source, start in x_sources:
+                lo = max(start, first)
+                hi = min(start + source.shape[3], first + X_CHUNK)
+                if lo < hi:
+                    nc.sync.dma_start(out=rows[:, :, lo - first : hi - first], in_=source[half, :, :, lo - start : hi - start])
+            return raw
+
+        def load_w1(g):
+            raw = w_raw_pool.tile([P, PACK, HIDDEN], BF16, name="w1_raw", tag="w_raw")
+            nc.sync.dma_start(
+                out=raw[:].rearrange("p (u e) w -> p u e w", u=2),
+                in_=rep_W1[g * K_PASS : (g + 1) * K_PASS, :].rearrange("(u p e) w -> p u e w", u=2, e=2),
+            )
+            return raw
+
+        def load_w2(g):
+            raw = w_raw_pool.tile([P, PACK, OUT], BF16, name="w2_raw", tag="w_raw")
+            nc.sync.dma_start(out=raw[:], in_=rep_W2[g * K_PASS : (g + 1) * K_PASS, :].rearrange("(t p) n -> p t n", t=PACK))
+            return raw
+
+        def transpose_chunk(raw, bank_set):
+            words = raw[:].bitcast(F32)
+            banks = []
+            for local in range(X_CHUNK // K_PASS):
+                for pair in range(SUB // 2):
+                    bank = psum.tile([P, 2, 2 * P], F32, name="x_bank", tag=bank_set)
+                    for u in range(2):
+                        for tt in range(2):
+                            first = (2 * pair + tt) * (X_CHUNK // 2) + local * WORDS + u * P
+                            nc.tensor.transpose(out=bank[:, u, tt * P : (tt + 1) * P], in_=words[:, first : first + P], identity=ident[:])
+                    banks.append(bank)
+            grouped_tiles = []
+            for local in range(X_CHUNK // K_PASS):
+                grouped = x_grp_pool.tile([P, HALF * PACK], BF16, name="x_grp", align_bytes=64)
+                word_pairs = grouped[:].bitcast(F32).rearrange("p (c u) -> p c u", u=2)
+                for pair in range(SUB // 2):
+                    nc.scalar.copy(
+                        out=word_pairs[:, pair * 2 * P : (pair + 1) * 2 * P, :],
+                        in_=banks[local * (SUB // 2) + pair][:].rearrange("p u c -> p c u"),
+                    )
+                grouped_tiles.append(grouped)
+            return grouped_tiles
+
+        def quantise_x(half, g, grouped):
+            nc.vector.quantize_mx(out=x_codes[:, half, g, :].bitcast(FP8X4), scales=x_scales[:, half, g, :], in_=grouped[:])
+
+        def group_rows(copy, grouped, raw, cols):
+            copy(
+                out=grouped[:, cols, :].rearrange("p (c i) t -> p c t i", i=4),
+                in_=raw[:, :, cols].rearrange("p t (c i) -> p c t i", i=4),
+            )
+
+        def group_weight(raw, width):
+            grouped = w_grp_pool.tile([P, width, PACK], BF16, name="w_grp", tag="w_grp", align_bytes=64)
+            split = width * VECTOR_SHARE_16THS // 16
+            group_rows(nc.vector.tensor_copy, grouped, raw, slice(0, split))
+            group_rows(nc.scalar.copy, grouped, raw, slice(split, width))
+            return grouped
+
+        def quantise_weight(codes, scales, grouped, cols):
+            nc.vector.quantize_mx(
+                out=codes[:, cols].bitcast(FP8X4),
+                scales=scales[:, cols],
+                in_=grouped[:, cols, :].rearrange("p w t -> p (w t)"),
+            )
+
+        def open_groups(h_tiles, bank_set):
+            for h in h_tiles:
+                acc[h] = psum.tile([P, HALF], F32, name="acc", tag=bank_set)
+
+        def first_product(half, h_tiles, passes):
+            for g in passes:
+                for h in h_tiles:
+                    nc.tensor.matmul_mx(
+                        out=acc[h][:],
+                        lhsT=w1_codes[:, g, h * P : (h + 1) * P].bitcast(FP8X4),
+                        lhsT_scale=w1_scales[:, g, h * P : (h + 1) * P],
+                        rhs=x_codes[:, half, g, :].bitcast(FP8X4),
+                        rhs_scale=x_scales[:, half, g, :],
+                        start=(g == 0),
+                        stop=(g == PASSES1 - 1),
+                    )
+
+        def relu_out(hidden, h):
+            if h % 2 == 0:
+                nc.scalar.activation(out=hidden[:, h % PACK, :], in_=acc[h][:], func=ACT.Relu, bias=b1_col[:, h : h + 1], scale=1.0)
+            else:
+                nc.vector.tensor_scalar(
+                    out=hidden[:, h % PACK, :], in0=acc[h][:], scalar1=b1_col[:, h : h + 1], scalar2=0.0, op0=ALU.add, op1=ALU.max
+                )
+
+        def group_hidden(hidden):
+            grouped = hidden_pool.tile([P, HALF, PACK], BF16, name="h1_grp", align_bytes=64)
+            group_rows(nc.vector.tensor_copy, grouped, hidden, slice(0, HALF))
+            return grouped
+
+        def quantise_hidden(half, g, grouped):
+            cols = slice(half * HALF, (half + 1) * HALF)
+            nc.vector.quantize_mx(
+                out=h1_codes[:, g, cols].bitcast(FP8X4), scales=h1_scales[:, g, cols], in_=grouped[:].rearrange("p c t -> p (c t)")
+            )
+
+        def second_product(half, t):
+            rows = slice(half * HALF + t * P, half * HALF + (t + 1) * P)
+            result = result_pool.tile([P, OUT], F32, name="result")
+            for first, last in OUT_BANKS:
+                cols = slice(first, last)
+                bank = psum.tile([P, last - first], F32, name="out_bank", tag="y")
+                for g in range(PASSES2):
+                    nc.tensor.matmul_mx(
+                        out=bank[:],
+                        lhsT=h1_codes[:, g, rows].bitcast(FP8X4),
+                        lhsT_scale=h1_scales[:, g, rows],
+                        rhs=w2_codes[:, g, cols].bitcast(FP8X4),
+                        rhs_scale=w2_scales[:, g, cols],
+                        start=(g == 0),
+                        stop=(g == PASSES2 - 1),
+                    )
+                nc.vector.tensor_tensor(out=result[:, cols], in0=bank[:], in1=b2_all[:, cols], op=ALU.add)
+            root = result_pool.tile([P, LATENT], F32, name="root")
+            nc.scalar.activation(out=root[:], in_=result[:, LATENT:OUT], func=ACT.Sqrt)
+            nc.sync.dma_start(out=outputs[0][half, :, t, :], in_=result[:, 0:LATENT])
+            nc.sync.dma_start(out=outputs[1][half, :, t, :], in_=result[:, LATENT:OUT])
+            return result, root
+
+        def draw_sample(half, t, result, root):
+            noise = result_pool.tile([P, LATENT], F32, name="noise")
+            nc.vector.tensor_tensor(out=noise[:], in0=root[:], in1=eps_all[:, half, t, :], op=ALU.mult)
+            sample = result_pool.tile([P, LATENT], F32, name="sample")
+            nc.gpsimd.tensor_tensor(out=sample[:], in0=noise[:], in1=result[:, 0:LATENT], op=ALU.add)
+            nc.sync.dma_start(out=outputs[2][half, :, t, :], in_=sample[:])
+
+        def finish_half(half):
+            waiting = None
+            for t in range(SUB):
+                fresh = second_product(half, t)
+                if waiting is not None:
+                    draw_sample(half, t - 1, waiting[0], waiting[1])
+                waiting = fresh
+            draw_sample(half, SUB - 1, waiting[0], waiting[1])
+
+        ident = keep.tile([P, P], F32)
+        make_identity(nc, ident[:])
+        b1_rows = keep.tile([P, P], BF16)
+        nc.vector.memset(b1_rows[:], 0.0)
+        nc.sync.dma_start(out=b1_rows[0:H_TILES, :], in_=rep_b1.rearrange("(r m) -> r m", m=P))
+        b2_row = keep.tile([P, OUT], BF16)
+        nc.vector.memset(b2_row[:], 0.0)
+        nc.sync.dma_start(out=b2_row[0:1, :], in_=rep_b2.rearrange("(o n) -> o n", o=1))
+        ones = keep.tile([P, P], BF16)
+        nc.vector.memset(ones[:], 1.0)
+        one = keep.tile([P, 1], F32)
+        nc.vector.memset(one[:], 1.0)
+        one_root = keep.tile([P, 1], F32)
+        nc.scalar.activation(out=one_root[:], in_=one[:], func=ACT.Sqrt)
+
+        x_raw = {}
+        w_raw = {}
+        x_raw[(0, 0)] = load_x(0, 0)
+        w_raw[0] = load_w1(0)
+        w_raw[1] = load_w1(1)
+        x_raw[(0, 1)] = load_x(0, 1)
+        w_raw[2] = load_w1(2)
+        w_raw[3] = load_w1(3)
+        x_raw[(0, 2)] = load_x(0, 2)
+
+        b1_rows_f32 = keep.tile([P, P], F32)
+        nc.vector.tensor_copy(out=b1_rows_f32[:], in_=b1_rows[:])
+        b1_bank = psum.tile([P, P], F32, tag="y")
+        nc.tensor.transpose(out=b1_bank[:], in_=b1_rows_f32[:], identity=ident[:])
+        b1_col = keep.tile([P, H_TILES], F32)
+        nc.vector.tensor_copy(out=b1_col[:], in_=b1_bank[:, 0:H_TILES])
+        b2_all = keep.tile([P, OUT], F32)
+        for first, last in OUT_BANKS:
+            cols = slice(first, last)
+            b2_bank = psum.tile([P, last - first], F32, name="b2_bank", tag="y")
+            nc.tensor.matmul(out=b2_bank[:], lhsT=ones[:], rhs=b2_row[:, cols], start=True, stop=True)
+            nc.vector.tensor_copy(out=b2_all[:, cols], in_=b2_bank[:])
+
+        def leave_psum(h_tiles):
+            hidden = hidden_pool.tile([P, PACK, HALF], BF16, name="hidden")
+            for h in h_tiles:
+                relu_out(hidden, h)
+            return hidden
+
+        acc = {}
+        grouped_w = {}
+        grouped_x = transpose_chunk(x_raw[(0, 0)], "y")
+        for chunk in range(CHUNKS):
+            passes = (2 * chunk, 2 * chunk + 1)
+            for local, g in enumerate(passes):
+                quantise_x(0, g, grouped_x[local])
+                grouped_w[g] = group_weight(w_raw[g], HIDDEN)
+            if chunk == 0:
+                w_raw[4] = load_w1(4)
+                w_raw[5] = load_w1(5)
+            x_raw[(1, chunk)] = load_x(1, chunk)
+            if chunk + 1 < CHUNKS:
+                grouped_x = transpose_chunk(x_raw[(0, chunk + 1)], "y")
+            for g in passes:
+                quantise_weight(w1_codes[:, g, :], w1_scales[:, g, :], grouped_w[g], slice(0, HIDDEN))
+            if chunk == 0:
+                open_groups(LOW, "x")
+            if chunk + 1 < CHUNKS:
+                first_product(0, LOW, passes)
+            else:
+                open_groups(HIGH, "y")
+                first_product(0, HIGH, range(passes[0]))
+                first_product(0, LOW + HIGH, passes)
+        w2_raw = (load_w2(0), load_w2(1))
+        eps_all = keep.tile([P, HALVES, SUB, LATENT], BF16)
+        nc.sync.dma_start(out=eps_all[:], in_=eps.rearrange("(h p t) c -> p h t c", h=HALVES, t=SUB))
+
+        hidden_low = leave_psum(LOW)
+        hidden_high = leave_psum(HIGH)
+        grouped_x = transpose_chunk(x_raw[(1, 0)], "x") + transpose_chunk(x_raw[(1, 1)], "x")
+        quantise_x(1, 0, grouped_x[0])
+        grouped_h = group_hidden(hidden_low)
+        quantise_x(1, 1, grouped_x[1])
+        quantise_hidden(0, 0, grouped_h)
+        open_groups(LOW, "y")
+        first_product(1, LOW, (0, 1))
+        grouped_x = grouped_x + transpose_chunk(x_raw[(1, 2)], "x")
+        quantise_x(1, 2, grouped_x[2])
+        grouped_h = group_hidden(hidden_high)
+        quantise_x(1, 3, grouped_x[3])
+        quantise_hidden(0, 1, grouped_h)
+        first_product(1, LOW, (2, 3))
+        for g in range(PASSES2):
+            grouped_w[g] = group_weight(w2_raw[g], OUT)
+            quantise_x(1, 4 + g, grouped_x[4 + g])
+        for g in range(PASSES2):
+            for first, last in OUT_BANKS:
+                quantise_weight(w2_codes[:, g, :], w2_scales[:, g, :], grouped_w[g], slice(first, last))
+        first_product(1, LOW, (4, 5))
+        hidden_low = leave_psum(LOW)
+
+        open_groups((4, 5), "x")
+        first_product(1, (4,), range(PASSES1))
+        first_product(1, (5,), range(PASSES1))
+        grouped_h = group_hidden(hidden_low)
+        hidden_high = hidden_pool.tile([P, PACK, HALF], BF16, name="hidden")
+        relu_out(hidden_high, 4)
+        relu_out(hidden_high, 5)
+        quantise_hidden(1, 0, grouped_h)
+        finish_half(0)
+        open_groups((6, 7), "x")
+        first_product(1, (6,), range(PASSES1))
+        first_product(1, (7,), range(PASSES1))
+        relu_out(hidden_high, 6)
+        relu_out(hidden_high, 7)
+        grouped_h = group_hidden(hidden_high)
+        quantise_hidden(1, 1, grouped_h)
+        finish_half(1)

@@ -23,6 +23,7 @@ PASSES2 = HIDDEN // K_PASS
 
 HALF = 512
 HALVES = BATCH // HALF
+QUARTER = HALF // 2
 SUB = HALF // P
 X_CHUNK = 2 * K_PASS
 CHUNKS = K1 // X_CHUNK
@@ -31,10 +32,11 @@ WORDS = K_PASS // 2
 H_TILES = HIDDEN // P
 LOW = (0, 1, 2, 3)
 HIGH = (4, 5, 6, 7)
+W_BUFS = 4
 
 OUT_BANKS = ((0, HALF), (HALF, OUT))
 
-VECTOR_SHARE_16THS = 9
+VECTOR_SHARE_16THS = 8
 
 FLOPS = 2 * BATCH * K1 * HIDDEN + 2 * BATCH * HIDDEN * OUT
 
@@ -48,7 +50,7 @@ def tile_rssm_pa_kernel(
         keep = ctx.enter_context(tc.tile_pool(name="keep", bufs=1))
         x_raw_pool = ctx.enter_context(tc.tile_pool(name="x_raw", bufs=3))
         x_grp_pool = ctx.enter_context(tc.tile_pool(name="x_grp", bufs=4))
-        w_raw_pool = ctx.enter_context(tc.tile_pool(name="w_raw", bufs=4))
+        w_raw_pool = ctx.enter_context(tc.tile_pool(name="w_raw", bufs=W_BUFS))
         w_grp_pool = ctx.enter_context(tc.tile_pool(name="w_grp", bufs=2))
         hidden_pool = ctx.enter_context(tc.tile_pool(name="hidden", bufs=2))
         result_pool = ctx.enter_context(tc.tile_pool(name="result", bufs=3))
@@ -139,48 +141,48 @@ def tile_rssm_pa_kernel(
                 in_=grouped[:, cols, :].rearrange("p w t -> p (w t)"),
             )
 
-        def open_groups(h_tiles, bank_set):
+        def open_groups(h_tiles, bank_set, width):
             for h in h_tiles:
-                acc[h] = psum.tile([P, HALF], F32, name="acc", tag=bank_set)
+                acc[h] = psum.tile([P, width], F32, name="acc", tag=bank_set)
 
-        def first_product(half, h_tiles, passes):
+        def first_product(half, h_tiles, passes, cols):
             for g in passes:
                 for h in h_tiles:
                     nc.tensor.matmul_mx(
                         out=acc[h][:],
                         lhsT=w1_codes[:, g, h * P : (h + 1) * P].bitcast(FP8X4),
                         lhsT_scale=w1_scales[:, g, h * P : (h + 1) * P],
-                        rhs=x_codes[:, half, g, :].bitcast(FP8X4),
-                        rhs_scale=x_scales[:, half, g, :],
+                        rhs=x_codes[:, half, g, cols].bitcast(FP8X4),
+                        rhs_scale=x_scales[:, half, g, cols],
                         start=(g == 0),
                         stop=(g == PASSES1 - 1),
                     )
 
-        def relu_out(hidden, h):
-            if h % 2 == 0:
-                nc.scalar.activation(out=hidden[:, h % PACK, :], in_=acc[h][:], func=ACT.Relu, bias=b1_col[:, h : h + 1], scale=1.0)
-            else:
+        def relu_out(hidden, h, on_vector):
+            if on_vector:
                 nc.vector.tensor_scalar(
                     out=hidden[:, h % PACK, :], in0=acc[h][:], scalar1=b1_col[:, h : h + 1], scalar2=0.0, op0=ALU.add, op1=ALU.max
                 )
+            else:
+                nc.scalar.activation(out=hidden[:, h % PACK, :], in_=acc[h][:], func=ACT.Relu, bias=b1_col[:, h : h + 1], scale=1.0)
 
-        def group_hidden(hidden):
-            grouped = hidden_pool.tile([P, HALF, PACK], BF16, name="h1_grp", align_bytes=64)
-            group_rows(nc.vector.tensor_copy, grouped, hidden, slice(0, HALF))
+        def group_hidden(hidden, width):
+            grouped = hidden_pool.tile([P, width, PACK], BF16, name="h1_grp", align_bytes=64)
+            group_rows(nc.vector.tensor_copy, grouped, hidden, slice(0, width))
             return grouped
 
-        def quantise_hidden(half, g, grouped):
-            cols = slice(half * HALF, (half + 1) * HALF)
+        def quantise_hidden(g, first_row, width, grouped):
+            cols = slice(first_row, first_row + width)
             nc.vector.quantize_mx(
                 out=h1_codes[:, g, cols].bitcast(FP8X4), scales=h1_scales[:, g, cols], in_=grouped[:].rearrange("p c t -> p (c t)")
             )
 
-        def second_product(half, t):
+        def second_product(half, t, bank_set):
             rows = slice(half * HALF + t * P, half * HALF + (t + 1) * P)
             result = result_pool.tile([P, OUT], F32, name="result")
             for first, last in OUT_BANKS:
                 cols = slice(first, last)
-                bank = psum.tile([P, last - first], F32, name="out_bank", tag="y")
+                bank = psum.tile([P, last - first], F32, name="out_bank", tag=bank_set)
                 for g in range(PASSES2):
                     nc.tensor.matmul_mx(
                         out=bank[:],
@@ -205,10 +207,10 @@ def tile_rssm_pa_kernel(
             nc.gpsimd.tensor_tensor(out=sample[:], in0=noise[:], in1=result[:, 0:LATENT], op=ALU.add)
             nc.sync.dma_start(out=outputs[2][half, :, t, :], in_=sample[:])
 
-        def finish_half(half):
+        def finish_half(half, bank_set):
             waiting = None
             for t in range(SUB):
-                fresh = second_product(half, t)
+                fresh = second_product(half, t, bank_set)
                 if waiting is not None:
                     draw_sample(half, t - 1, waiting[0], waiting[1])
                 waiting = fresh
@@ -231,13 +233,10 @@ def tile_rssm_pa_kernel(
 
         x_raw = {}
         w_raw = {}
-        x_raw[(0, 0)] = load_x(0, 0)
-        w_raw[0] = load_w1(0)
-        w_raw[1] = load_w1(1)
-        x_raw[(0, 1)] = load_x(0, 1)
-        w_raw[2] = load_w1(2)
-        w_raw[3] = load_w1(3)
-        x_raw[(0, 2)] = load_x(0, 2)
+        for chunk in range(CHUNKS):
+            x_raw[(0, chunk)] = load_x(0, chunk)
+        for g in range(W_BUFS):
+            w_raw[g] = load_w1(g)
 
         b1_rows_f32 = keep.tile([P, P], F32)
         nc.vector.tensor_copy(out=b1_rows_f32[:], in_=b1_rows[:])
@@ -252,78 +251,81 @@ def tile_rssm_pa_kernel(
             nc.tensor.matmul(out=b2_bank[:], lhsT=ones[:], rhs=b2_row[:, cols], start=True, stop=True)
             nc.vector.tensor_copy(out=b2_all[:, cols], in_=b2_bank[:])
 
-        def leave_psum(h_tiles):
+        def leave_psum(h_tiles, share_with_vector):
             hidden = hidden_pool.tile([P, PACK, HALF], BF16, name="hidden")
             for h in h_tiles:
-                relu_out(hidden, h)
+                relu_out(hidden, h, share_with_vector and h % 2 == 1)
             return hidden
+
+        whole = slice(0, HALF)
 
         acc = {}
         grouped_w = {}
-        grouped_x = transpose_chunk(x_raw[(0, 0)], "y")
+        waiting = None
         for chunk in range(CHUNKS):
-            passes = (2 * chunk, 2 * chunk + 1)
-            for local, g in enumerate(passes):
-                quantise_x(0, g, grouped_x[local])
+            fresh = transpose_chunk(x_raw[(0, chunk)], ("y", "x")[chunk % 2])
+            if waiting is not None:
+                quantise_x(0, 2 * chunk - 2, waiting[0])
+                quantise_x(0, 2 * chunk - 1, waiting[1])
+            waiting = fresh
+        quantise_x(0, 2 * CHUNKS - 2, waiting[0])
+        quantise_x(0, 2 * CHUNKS - 1, waiting[1])
+
+        open_groups(LOW, "x", HALF)
+        open_groups(HIGH, "y", HALF)
+        w2_raw = []
+        for g in range(PASSES1 + 1):
+            if g > 0:
+                quantise_weight(w1_codes[:, g - 1, :], w1_scales[:, g - 1, :], grouped_w[g - 1], slice(0, HIDDEN))
+                first_product(0, LOW + HIGH, (g - 1,), whole)
+            if g < PASSES1:
                 grouped_w[g] = group_weight(w_raw[g], HIDDEN)
-            if chunk == 0:
-                w_raw[4] = load_w1(4)
-                w_raw[5] = load_w1(5)
+            if g + W_BUFS < PASSES1:
+                w_raw[g + W_BUFS] = load_w1(g + W_BUFS)
+            elif g + W_BUFS < PASSES1 + PASSES2:
+                w2_raw.append(load_w2(g + W_BUFS - PASSES1))
+        for chunk in range(CHUNKS):
             x_raw[(1, chunk)] = load_x(1, chunk)
-            if chunk + 1 < CHUNKS:
-                grouped_x = transpose_chunk(x_raw[(0, chunk + 1)], "y")
-            for g in passes:
-                quantise_weight(w1_codes[:, g, :], w1_scales[:, g, :], grouped_w[g], slice(0, HIDDEN))
-            if chunk == 0:
-                open_groups(LOW, "x")
-            if chunk + 1 < CHUNKS:
-                first_product(0, LOW, passes)
-            else:
-                open_groups(HIGH, "y")
-                first_product(0, HIGH, range(passes[0]))
-                first_product(0, LOW + HIGH, passes)
-        w2_raw = (load_w2(0), load_w2(1))
         eps_all = keep.tile([P, HALVES, SUB, LATENT], BF16)
         nc.sync.dma_start(out=eps_all[:], in_=eps.rearrange("(h p t) c -> p h t c", h=HALVES, t=SUB))
 
-        hidden_low = leave_psum(LOW)
-        hidden_high = leave_psum(HIGH)
-        grouped_x = transpose_chunk(x_raw[(1, 0)], "x") + transpose_chunk(x_raw[(1, 1)], "x")
-        quantise_x(1, 0, grouped_x[0])
-        grouped_h = group_hidden(hidden_low)
-        quantise_x(1, 1, grouped_x[1])
-        quantise_hidden(0, 0, grouped_h)
-        open_groups(LOW, "y")
-        first_product(1, LOW, (0, 1))
-        grouped_x = grouped_x + transpose_chunk(x_raw[(1, 2)], "x")
-        quantise_x(1, 2, grouped_x[2])
-        grouped_h = group_hidden(hidden_high)
-        quantise_x(1, 3, grouped_x[3])
-        quantise_hidden(0, 1, grouped_h)
-        first_product(1, LOW, (2, 3))
         for g in range(PASSES2):
             grouped_w[g] = group_weight(w2_raw[g], OUT)
-            quantise_x(1, 4 + g, grouped_x[4 + g])
+        hidden_low = leave_psum(LOW, True)
+        hidden_high = leave_psum(HIGH, True)
         for g in range(PASSES2):
             for first, last in OUT_BANKS:
                 quantise_weight(w2_codes[:, g, :], w2_scales[:, g, :], grouped_w[g], slice(first, last))
-        first_product(1, LOW, (4, 5))
-        hidden_low = leave_psum(LOW)
 
-        open_groups((4, 5), "x")
-        first_product(1, (4,), range(PASSES1))
-        first_product(1, (5,), range(PASSES1))
-        grouped_h = group_hidden(hidden_low)
-        hidden_high = hidden_pool.tile([P, PACK, HALF], BF16, name="hidden")
-        relu_out(hidden_high, 4)
-        relu_out(hidden_high, 5)
-        quantise_hidden(1, 0, grouped_h)
-        finish_half(0)
-        open_groups((6, 7), "x")
-        first_product(1, (6,), range(PASSES1))
-        first_product(1, (7,), range(PASSES1))
-        relu_out(hidden_high, 6)
-        relu_out(hidden_high, 7)
-        grouped_h = group_hidden(hidden_high)
-        quantise_hidden(1, 1, grouped_h)
-        finish_half(1)
+        grouped_x = transpose_chunk(x_raw[(1, 0)], "x") + transpose_chunk(x_raw[(1, 1)], "x")
+        quantise_x(1, 0, grouped_x[0])
+        grouped_h = group_hidden(hidden_low, HALF)
+        quantise_x(1, 1, grouped_x[1])
+        quantise_hidden(0, 0, HALF, grouped_h)
+        open_groups(LOW, "y", HALF)
+        first_product(1, LOW, (0, 1), whole)
+        grouped_x = grouped_x + transpose_chunk(x_raw[(1, 2)], "x")
+        quantise_x(1, 2, grouped_x[2])
+        grouped_h = group_hidden(hidden_high, HALF)
+        quantise_x(1, 3, grouped_x[3])
+        quantise_hidden(1, 0, HALF, grouped_h)
+        first_product(1, LOW, (2, 3), whole)
+        quantise_x(1, 4, grouped_x[4])
+        quantise_x(1, 5, grouped_x[5])
+        finish_half(0, "x")
+        first_product(1, LOW, (4, 5), whole)
+        hidden_low = leave_psum(LOW, False)
+
+        grouped_q = {}
+        for quarter, bank_set in enumerate(("y", "x")):
+            hidden_high = hidden_pool.tile([P, PACK, QUARTER], BF16, name="hidden_q")
+            for h in HIGH:
+                open_groups((h,), bank_set, QUARTER)
+                first_product(1, (h,), range(PASSES1), slice(quarter * QUARTER, (quarter + 1) * QUARTER))
+                relu_out(hidden_high, h, False)
+            if quarter == 0:
+                grouped_h = group_hidden(hidden_low, HALF)
+                quantise_hidden(0, HALF, HALF, grouped_h)
+            grouped_q[quarter] = group_hidden(hidden_high, QUARTER)
+            quantise_hidden(1, HALF + quarter * QUARTER, QUARTER, grouped_q[quarter])
+        finish_half(1, "y")

@@ -46,7 +46,6 @@ def tile_rssm_pa_kernel(
 ):
     nc = tc.nc
     with ExitStack() as ctx:
-        ctx.enter_context(tc.manual_schedule())
         keep = ctx.enter_context(tc.tile_pool(name="keep", bufs=1))
         x_raw_pool = ctx.enter_context(tc.tile_pool(name="x_raw", bufs=3))
         x_grp_pool = ctx.enter_context(tc.tile_pool(name="x_grp", bufs=4))

from contextlib import ExitStack

import concourse.mybir as mybir
from concourse.masks import make_identity

F32 = mybir.dt.float32
BF16 = mybir.dt.bfloat16
U32 = mybir.dt.uint32
U8 = mybir.dt.uint8
FP8X4 = mybir.dt.float8_e4m3fn_x4
ACT = mybir.ActivationFunctionType
ALU = mybir.AluOpType

P = 128
PACK = 4
K_PASS = P * PACK

BATCH, STATE, ACTION, OBS, HIDDEN, LATENT = 1024, 1024, 128, 1920, 1024, 384
K1 = STATE + ACTION + OBS
OUT = 2 * LATENT
PASSES1 = K1 // K_PASS
PASSES2 = HIDDEN // K_PASS

HALF = 512
HALVES = BATCH // HALF
QUARTER = HALF // 2
SUB = HALF // P
X_CHUNK = 2 * K_PASS
CHUNKS = K1 // X_CHUNK
WORDS = K_PASS // 2

H_TILES = HIDDEN // P
LOW = (0, 1, 2, 3)
HIGH = (4, 5, 6, 7)
W_BUFS = 4

OUT_BANKS = ((0, HALF), (HALF, OUT))

VECTOR_SHARE_16THS = 8

FLOPS = 2 * BATCH * K1 * HIDDEN + 2 * BATCH * HIDDEN * OUT


def tile_rssm_pa_kernel(
    tc, prev_state, prev_action, observation, eps, rep_W1, rep_b1, rep_W2, rep_b2, out_0, out_1, out_2
):
    nc = tc.nc
    with ExitStack() as ctx:
        keep = ctx.enter_context(tc.tile_pool(name="keep", bufs=1))
        x_raw_pool = ctx.enter_context(tc.tile_pool(name="x_raw", bufs=3))
        x_grp_pool = ctx.enter_context(tc.tile_pool(name="x_grp", bufs=4))
        w_raw_pool = ctx.enter_context(tc.tile_pool(name="w_raw", bufs=W_BUFS))
        w_grp_pool = ctx.enter_context(tc.tile_pool(name="w_grp", bufs=2))
        hidden_pool = ctx.enter_context(tc.tile_pool(name="hidden", bufs=2))
        result_pool = ctx.enter_context(tc.tile_pool(name="result", bufs=3))
        psum = ctx.enter_context(tc.psum_pool(name="psum", bufs=4))

        def by_tile(dram):
            return dram.rearrange("(h p t) c -> h p t c", h=HALVES, t=SUB)

        x_sources = ((by_tile(prev_state), 0), (by_tile(prev_action), STATE), (by_tile(observation), STATE + ACTION))
        outputs = (by_tile(out_0), by_tile(out_1), by_tile(out_2))

        x_codes = keep.tile([P, HALVES, PASSES1, HALF], U32, align_bytes=64)
        x_scales = keep.tile([P, HALVES, PASSES1, HALF], U8, align_bytes=64)
        w1_codes = keep.tile([P, PASSES1, HIDDEN], U32, align_bytes=64)
        w1_scales = keep.tile([P, PASSES1, HIDDEN], U8, align_bytes=64)
        h1_codes = keep.tile([P, PASSES2, BATCH], U32, align_bytes=64)
        h1_scales = keep.tile([P, PASSES2, BATCH], U8, align_bytes=64)
        w2_codes = keep.tile([P, PASSES2, OUT], U32, align_bytes=64)
        w2_scales = keep.tile([P, PASSES2, OUT], U8, align_bytes=64)

        def load_x(half, chunk):
            raw = x_raw_pool.tile([P, SUB * X_CHUNK], BF16, name="x_raw")
            rows = raw[:].rearrange("p (t k) -> p t k", t=SUB)
            first = chunk * X_CHUNK
            for source, start in x_sources:
                lo = max(start, first)
                hi = min(start + source.shape[3], first + X_CHUNK)
                if lo < hi:
                    nc.sync.dma_start(out=rows[:, :, lo - first : hi - first], in_=source[half, :, :, lo - start : hi - start])
            return raw

        def load_w1(g):
            raw = w_raw_pool.tile([P, PACK, HIDDEN], BF16, name="w1_raw", tag="w_raw")
            nc.sync.dma_start(
                out=raw[:].rearrange("p (u e) w -> p u e w", u=2),
                in_=rep_W1[g * K_PASS : (g + 1) * K_PASS, :].rearrange("(u p e) w -> p u e w", u=2, e=2),
            )
            return raw

        def load_w2(g):
            raw = w_raw_pool.tile([P, PACK, OUT], BF16, name="w2_raw", tag="w_raw")
            nc.sync.dma_start(out=raw[:], in_=rep_W2[g * K_PASS : (g + 1) * K_PASS, :].rearrange("(t p) n -> p t n", t=PACK))
            return raw

        def transpose_chunk(raw, bank_set):
            words = raw[:].bitcast(F32)
            banks = []
            for local in range(X_CHUNK // K_PASS):
                for pair in range(SUB // 2):
                    bank = psum.tile([P, 2, 2 * P], F32, name="x_bank", tag=bank_set)
                    for u in range(2):
                        for tt in range(2):
                            first = (2 * pair + tt) * (X_CHUNK // 2) + local * WORDS + u * P
                            nc.tensor.transpose(out=bank[:, u, tt * P : (tt + 1) * P], in_=words[:, first : first + P], identity=ident[:])
                    banks.append(bank)
            grouped_tiles = []
            for local in range(X_CHUNK // K_PASS):
                grouped = x_grp_pool.tile([P, HALF * PACK], BF16, name="x_grp", align_bytes=64)
                word_pairs = grouped[:].bitcast(F32).rearrange("p (c u) -> p c u", u=2)
                for pair in range(SUB // 2):
                    nc.scalar.copy(
                        out=word_pairs[:, pair * 2 * P : (pair + 1) * 2 * P, :],
                        in_=banks[local * (SUB // 2) + pair][:].rearrange("p u c -> p c u"),
                    )
                grouped_tiles.append(grouped)
            return grouped_tiles

        def quantise_x(half, g, grouped):
            nc.vector.quantize_mx(out=x_codes[:, half, g, :].bitcast(FP8X4), scales=x_scales[:, half, g, :], in_=grouped[:])

        def group_rows(copy, grouped, raw, cols):
            copy(
                out=grouped[:, cols, :].rearrange("p (c i) t -> p c t i", i=4),
                in_=raw[:, :, cols].rearrange("p t (c i) -> p c t i", i=4),
            )

        def group_weight(raw, width):
            grouped = w_grp_pool.tile([P, width, PACK], BF16, name="w_grp", tag="w_grp", align_bytes=64)
            split = width * VECTOR_SHARE_16THS // 16
            group_rows(nc.vector.tensor_copy, grouped, raw, slice(0, split))
            group_rows(nc.scalar.copy, grouped, raw, slice(split, width))
            return grouped

        def quantise_weight(codes, scales, grouped, cols):
            nc.vector.quantize_mx(
                out=codes[:, cols].bitcast(FP8X4),
                scales=scales[:, cols],
                in_=grouped[:, cols, :].rearrange("p w t -> p (w t)"),
            )

        def open_groups(h_tiles, bank_set, width):
            for h in h_tiles:
                acc[h] = psum.tile([P, width], F32, name="acc", tag=bank_set)

        def first_product(half, h_tiles, passes, cols):
            for g in passes:
                for h in h_tiles:
                    nc.tensor.matmul_mx(
                        out=acc[h][:],
                        lhsT=w1_codes[:, g, h * P : (h + 1) * P].bitcast(FP8X4),
                        lhsT_scale=w1_scales[:, g, h * P : (h + 1) * P],
                        rhs=x_codes[:, half, g, cols].bitcast(FP8X4),
                        rhs_scale=x_scales[:, half, g, cols],
                        start=(g == 0),
                        stop=(g == PASSES1 - 1),
                    )

        def relu_out(hidden, h, on_vector):
            if on_vector:
                nc.vector.tensor_scalar(
                    out=hidden[:, h % PACK, :], in0=acc[h][:], scalar1=b1_col[:, h : h + 1], scalar2=0.0, op0=ALU.add, op1=ALU.max
                )
            else:
                nc.scalar.activation(out=hidden[:, h % PACK, :], in_=acc[h][:], func=ACT.Relu, bias=b1_col[:, h : h + 1], scale=1.0)

        def group_hidden(hidden, width):
            grouped = hidden_pool.tile([P, width, PACK], BF16, name="h1_grp", align_bytes=64)
            group_rows(nc.vector.tensor_copy, grouped, hidden, slice(0, width))
            return grouped

        def quantise_hidden(g, first_row, width, grouped):
            cols = slice(first_row, first_row + width)
            nc.vector.quantize_mx(
                out=h1_codes[:, g, cols].bitcast(FP8X4), scales=h1_scales[:, g, cols], in_=grouped[:].rearrange("p c t -> p (c t)")
            )

        def second_product(half, t, bank_set):
            rows = slice(half * HALF + t * P, half * HALF + (t + 1) * P)
            result = result_pool.tile([P, OUT], F32, name="result")
            for first, last in OUT_BANKS:
                cols = slice(first, last)
                bank = psum.tile([P, last - first], F32, name="out_bank", tag=bank_set)
                for g in range(PASSES2):
                    nc.tensor.matmul_mx(
                        out=bank[:],
                        lhsT=h1_codes[:, g, rows].bitcast(FP8X4),
                        lhsT_scale=h1_scales[:, g, rows],
                        rhs=w2_codes[:, g, cols].bitcast(FP8X4),
                        rhs_scale=w2_scales[:, g, cols],
                        start=(g == 0),
                        stop=(g == PASSES2 - 1),
                    )
                nc.vector.tensor_tensor(out=result[:, cols], in0=bank[:], in1=b2_all[:, cols], op=ALU.add)
            root = result_pool.tile([P, LATENT], F32, name="root")
            nc.scalar.activation(out=root[:], in_=result[:, LATENT:OUT], func=ACT.Sqrt)
            nc.sync.dma_start(out=outputs[0][half, :, t, :], in_=result[:, 0:LATENT])
            nc.sync.dma_start(out=outputs[1][half, :, t, :], in_=result[:, LATENT:OUT])
            return result, root

        def draw_sample(half, t, result, root):
            noise = result_pool.tile([P, LATENT], F32, name="noise")
            nc.vector.tensor_tensor(out=noise[:], in0=root[:], in1=eps_all[:, half, t, :], op=ALU.mult)
            sample = result_pool.tile([P, LATENT], F32, name="sample")
            nc.gpsimd.tensor_tensor(out=sample[:], in0=noise[:], in1=result[:, 0:LATENT], op=ALU.add)
            nc.sync.dma_start(out=outputs[2][half, :, t, :], in_=sample[:])

        def finish_half(half, bank_set):
            waiting = None
            for t in range(SUB):
                fresh = second_product(half, t, bank_set)
                if waiting is not None:
                    draw_sample(half, t - 1, waiting[0], waiting[1])
                waiting = fresh
            draw_sample(half, SUB - 1, waiting[0], waiting[1])

        ident = keep.tile([P, P], F32)
        make_identity(nc, ident[:])
        b1_rows = keep.tile([P, P], BF16)
        nc.vector.memset(b1_rows[:], 0.0)
        nc.sync.dma_start(out=b1_rows[0:H_TILES, :], in_=rep_b1.rearrange("(r m) -> r m", m=P))
        b2_row = keep.tile([P, OUT], BF16)
        nc.vector.memset(b2_row[:], 0.0)
        nc.sync.dma_start(out=b2_row[0:1, :], in_=rep_b2.rearrange("(o n) -> o n", o=1))
        ones = keep.tile([P, P], BF16)
        nc.vector.memset(ones[:], 1.0)
        one = keep.tile([P, 1], F32)
        nc.vector.memset(one[:], 1.0)
        one_root = keep.tile([P, 1], F32)
        nc.scalar.activation(out=one_root[:], in_=one[:], func=ACT.Sqrt)

        x_raw = {}
        w_raw = {}
        for chunk in range(CHUNKS):
            x_raw[(0, chunk)] = load_x(0, chunk)
        for g in range(W_BUFS):
            w_raw[g] = load_w1(g)

        b1_rows_f32 = keep.tile([P, P], F32)
        nc.vector.tensor_copy(out=b1_rows_f32[:], in_=b1_rows[:])
        b1_bank = psum.tile([P, P], F32, tag="y")
        nc.tensor.transpose(out=b1_bank[:], in_=b1_rows_f32[:], identity=ident[:])
        b1_col = keep.tile([P, H_TILES], F32)
        nc.vector.tensor_copy(out=b1_col[:], in_=b1_bank[:, 0:H_TILES])
        b2_all = keep.tile([P, OUT], F32)
        for first, last in OUT_BANKS:
            cols = slice(first, last)
            b2_bank = psum.tile([P, last - first], F32, name="b2_bank", tag="y")
            nc.tensor.matmul(out=b2_bank[:], lhsT=ones[:], rhs=b2_row[:, cols], start=True, stop=True)
            nc.vector.tensor_copy(out=b2_all[:, cols], in_=b2_bank[:])

        def leave_psum(h_tiles, share_with_vector):
            hidden = hidden_pool.tile([P, PACK, HALF], BF16, name="hidden")
            for h in h_tiles:
                relu_out(hidden, h, share_with_vector and h % 2 == 1)
            return hidden

        whole = slice(0, HALF)

        acc = {}
        grouped_w = {}
        waiting = None
        for chunk in range(CHUNKS):
            fresh = transpose_chunk(x_raw[(0, chunk)], ("y", "x")[chunk % 2])
            if waiting is not None:
                quantise_x(0, 2 * chunk - 2, waiting[0])
                quantise_x(0, 2 * chunk - 1, waiting[1])
            waiting = fresh
        quantise_x(0, 2 * CHUNKS - 2, waiting[0])
        quantise_x(0, 2 * CHUNKS - 1, waiting[1])

        open_groups(LOW, "x", HALF)
        open_groups(HIGH, "y", HALF)
        w2_raw = []
        for g in range(PASSES1 + 1):
            if g > 0:
                quantise_weight(w1_codes[:, g - 1, :], w1_scales[:, g - 1, :], grouped_w[g - 1], slice(0, HIDDEN))
                first_product(0, LOW + HIGH, (g - 1,), whole)
            if g < PASSES1:
                grouped_w[g] = group_weight(w_raw[g], HIDDEN)
            if g + W_BUFS < PASSES1:
                w_raw[g + W_BUFS] = load_w1(g + W_BUFS)
            elif g + W_BUFS < PASSES1 + PASSES2:
                w2_raw.append(load_w2(g + W_BUFS - PASSES1))
        for chunk in range(CHUNKS):
            x_raw[(1, chunk)] = load_x(1, chunk)
        eps_all = keep.tile([P, HALVES, SUB, LATENT], BF16)
        nc.sync.dma_start(out=eps_all[:], in_=eps.rearrange("(h p t) c -> p h t c", h=HALVES, t=SUB))

        for g in range(PASSES2):
            grouped_w[g] = group_weight(w2_raw[g], OUT)
        hidden_low = leave_psum(LOW, True)
        hidden_high = leave_psum(HIGH, True)
        for g in range(PASSES2):
            for first, last in OUT_BANKS:
                quantise_weight(w2_codes[:, g, :], w2_scales[:, g, :], grouped_w[g], slice(first, last))

        grouped_x = transpose_chunk(x_raw[(1, 0)], "x") + transpose_chunk(x_raw[(1, 1)], "x")
        quantise_x(1, 0, grouped_x[0])
        grouped_h = group_hidden(hidden_low, HALF)
        quantise_x(1, 1, grouped_x[1])
        quantise_hidden(0, 0, HALF, grouped_h)
        open_groups(LOW, "y", HALF)
        first_product(1, LOW, (0, 1), whole)
        grouped_x = grouped_x + transpose_chunk(x_raw[(1, 2)], "x")
        quantise_x(1, 2, grouped_x[2])
        grouped_h = group_hidden(hidden_high, HALF)
        quantise_x(1, 3, grouped_x[3])
        quantise_hidden(1, 0, HALF, grouped_h)
        first_product(1, LOW, (2, 3), whole)
        quantise_x(1, 4, grouped_x[4])
        quantise_x(1, 5, grouped_x[5])
        finish_half(0, "x")
        first_product(1, LOW, (4, 5), whole)
        hidden_low = leave_psum(LOW, False)

        grouped_q = {}
        for quarter, bank_set in enumerate(("y", "x")):
            hidden_high = hidden_pool.tile([P, PACK, QUARTER], BF16, name="hidden_q")
            for h in HIGH:
                open_groups((h,), bank_set, QUARTER)
                first_product(1, (h,), range(PASSES1), slice(quarter * QUARTER, (quarter + 1) * QUARTER))
                relu_out(hidden_high, h, False)
            if quarter == 0:
                grouped_h = group_hidden(hidden_low, HALF)
                quantise_hidden(0, HALF, HALF, grouped_h)
            grouped_q[quarter] = group_hidden(hidden_high, QUARTER)
            quantise_hidden(1, HALF + quarter * QUARTER, QUARTER, grouped_q[quarter])
        finish_half(1, "y")
